import numpy as np
import ml_dtypes

BF16 = ml_dtypes.bfloat16


def bf(x):
    return np.asarray(x, np.float32).astype(BF16)


def f32(x):
    return np.asarray(x, np.float32)


def f64(x):
    return np.asarray(x).astype(np.float64)


def striped(idx):
    return np.tile(idx.reshape(-1, 16).T, (8, 1))


V, A, H, NH, N = 512, 128, 256, 2, 128


def setup_inputs():
    return {
        "table": bf(np.random.standard_normal((A, V))),
        "dr_w": bf(np.random.standard_normal((A, H)) / np.sqrt(A)),
        "dr_b": f32(0.2 * np.random.standard_normal((H, 1))),
        "w2": bf(np.random.standard_normal((H, NH * H)) / np.sqrt(H)),
        "w2_b": f32(0.2 * np.random.standard_normal((NH * H, 1))),
        "offs": striped(np.random.permutation(np.tile(np.arange(V), 2))[:N]),
    }


def reference(table, dr_w, dr_b, w2, w2_b, offs):
    idx = offs[:16].T.reshape(-1)
    fea = np.maximum(f64(dr_w).T @ f64(table)[:, idx] + f64(dr_b), 0.0)
    q = f64(w2).T @ fea + f64(w2_b)
    return np.concatenate([fea, q], axis=0)

@@ -1,0 +1,75 @@
+import concourse.mybir as mybir
+
+BF16, F32, U16 = mybir.dt.bfloat16, mybir.dt.float32, mybir.dt.uint16
+ADD, MAX = mybir.AluOpType.add, mybir.AluOpType.max
+RELU, IDENTITY = mybir.ActivationFunctionType.Relu, mybir.ActivationFunctionType.Identity
+
+P = 128
+V = 512
+N = 128
+H = 256
+R = 512
+H_BLOCKS = H // P
+R_BLOCKS = R // P
+
+FLOPS = 2 * P * H * N + 2 * H * R * N
+
+
+def add_bias(nc, block, dst, src, bias, relu):
+    if block % 2 == 0:
+        if relu:
+            nc.vector.tensor_scalar(dst, src, bias, 0.0, ADD, MAX)
+        else:
+            nc.vector.tensor_scalar(dst, src, bias, None, ADD)
+    else:
+        nc.scalar.activation(dst, src, RELU if relu else IDENTITY, bias=bias)
+
+
+def tile_mutiheadattn_kernel(tc, table, dr_w, dr_b, w2, w2_b, offs, out):
+    nc = tc.nc
+    with (
+        tc.tile_pool(name="held", bufs=1) as held,
+        tc.psum_pool(name="psum", bufs=1) as psum,
+    ):
+        offsets = held.tile([P, N // 16], U16, name="offsets")
+        table_sb = held.tile([P, V], BF16, name="table_sb")
+        dr_w_sb = held.tile([P, H], BF16, name="dr_w_sb")
+        dr_b_sb = held.tile([P, H_BLOCKS], F32, name="dr_b_sb")
+        w2_sb = held.tile([P, H_BLOCKS, R], BF16, name="w2_sb")
+        w2_b_sb = held.tile([P, R_BLOCKS], F32, name="w2_b_sb")
+        w2_blocks = w2.rearrange("(b p) r -> b p r", p=P)
+
+        nc.sync.dma_start(offsets[:], offs)
+        nc.scalar.dma_start(dr_w_sb[:], dr_w)
+        nc.sync.dma_start(table_sb[:], table)
+        with nc.allow_non_contiguous_dma(reason="a bias: one float32 to a partition"):
+            nc.scalar.dma_start(dr_b_sb[:], dr_b.rearrange("(b p) one -> p (b one)", p=P))
+        nc.sync.dma_start(w2_sb[:, 0, :], w2_blocks[0])
+        nc.scalar.dma_start(w2_sb[:, 1, :], w2_blocks[1])
+        with nc.allow_non_contiguous_dma(reason="a bias: one float32 to a partition"):
+            nc.scalar.dma_start(w2_b_sb[:], w2_b.rearrange("(c p) one -> p (c one)", p=P))
+
+        fea_bf16 = held.tile([P, H_BLOCKS, N], BF16, name="fea_bf16")
+        fea_f32 = held.tile([P, H_BLOCKS, N], F32, name="fea_f32")
+        for b in range(H_BLOCKS):
+            fea_ps = psum.tile([P, N], F32, name=f"fea_ps{b}")
+            nc.tensor.matmul(
+                fea_ps[:], dr_w_sb[:, b * P : (b + 1) * P], table_sb[:].indirect(offsets[:])
+            )
+            add_bias(nc, b, fea_bf16[:, b, :], fea_ps[:], dr_b_sb[:, b : b + 1], relu=True)
+            add_bias(nc, b, fea_f32[:, b, :], fea_ps[:], dr_b_sb[:, b : b + 1], relu=True)
+        nc.sync.dma_start(out[0:H, :].rearrange("(b p) j -> p b j", p=P), fea_f32[:])
+
+        q_f32 = held.tile([P, R_BLOCKS, N], F32, name="q_f32")
+        for c in range(R_BLOCKS):
+            q_ps = psum.tile([P, N], F32, name=f"q_ps{c}")
+            for b in range(H_BLOCKS):
+                nc.tensor.matmul(
+                    q_ps[:],
+                    w2_sb[:, b, c * P : (c + 1) * P],
+                    fea_bf16[:, b, :],
+                    start=(b == 0),
+                    stop=(b == H_BLOCKS - 1),
+                )
+            add_bias(nc, c, q_f32[:, c, :], q_ps[:], w2_b_sb[:, c : c + 1], relu=False)
+        nc.sync.dma_start(out[H : H + R, :].rearrange("(c p) j -> p c j", p=P), q_f32[:])

@@ -49,6 +49,10 @@ def tile_mutiheadattn_kernel(tc, table, dr_w, dr_b, w2, w2_b, offs, out):
         with nc.allow_non_contiguous_dma(reason="a bias: one float32 to a partition"):
             nc.scalar.dma_start(w2_b_sb[:], w2_b.rearrange("(c p) one -> p (c one)", p=P))
 
+        scratch = held.tile([P, 1], F32, name="scratch")
+        nc.vector.memset(scratch[:], 0.0)
+        nc.scalar.activation(scratch[:], scratch[:], RELU)
+
         fea_bf16 = held.tile([P, H_BLOCKS, N], BF16, name="fea_bf16")
         fea_f32 = held.tile([P, H_BLOCKS, N], F32, name="fea_f32")
         for b in range(H_BLOCKS):

@@ -62,18 +62,19 @@ def tile_mutiheadattn_kernel(tc, table, dr_w, dr_b, w2, w2_b, offs, out):
             )
             add_bias(nc, b, fea_bf16[:, b, :], fea_ps[:], dr_b_sb[:, b : b + 1], relu=True)
             add_bias(nc, b, fea_f32[:, b, :], fea_ps[:], dr_b_sb[:, b : b + 1], relu=True)
-        nc.sync.dma_start(out[0:H, :].rearrange("(b p) j -> p b j", p=P), fea_f32[:])
+            nc.sync.dma_start(out[b * P : (b + 1) * P, :], fea_f32[:, b, :])
 
         q_f32 = held.tile([P, R_BLOCKS, N], F32, name="q_f32")
-        for c in range(R_BLOCKS):
-            q_ps = psum.tile([P, N], F32, name=f"q_ps{c}")
-            for b in range(H_BLOCKS):
+        q_ps = [psum.tile([P, N], F32, name=f"q_ps{c}") for c in range(R_BLOCKS)]
+        for b in range(H_BLOCKS):
+            for c in range(R_BLOCKS):
                 nc.tensor.matmul(
-                    q_ps[:],
+                    q_ps[c][:],
                     w2_sb[:, b, c * P : (c + 1) * P],
                     fea_bf16[:, b, :],
                     start=(b == 0),
                     stop=(b == H_BLOCKS - 1),
                 )
-            add_bias(nc, c, q_f32[:, c, :], q_ps[:], w2_b_sb[:, c : c + 1], relu=False)
-        nc.sync.dma_start(out[H : H + R, :].rearrange("(c p) j -> p c j", p=P), q_f32[:])
+        for c in range(R_BLOCKS):
+            add_bias(nc, c, q_f32[:, c, :], q_ps[c][:], w2_b_sb[:, c : c + 1], relu=False)
+            nc.sync.dma_start(out[H + c * P : H + (c + 1) * P, :], q_f32[:, c, :])

@@ -11,6 +11,8 @@ H = 256
 R = 512
 H_BLOCKS = H // P
 R_BLOCKS = R // P
+BANK = 512
+WARM_UP_MATMULS = 6
 
 FLOPS = 2 * P * H * N + 2 * H * R * N
 
@@ -52,6 +54,12 @@ def tile_mutiheadattn_kernel(tc, table, dr_w, dr_b, w2, w2_b, offs, out):
         scratch = held.tile([P, 1], F32, name="scratch")
         nc.vector.memset(scratch[:], 0.0)
         nc.scalar.activation(scratch[:], scratch[:], RELU)
+
+        zeros = held.tile([P, BANK], BF16, name="zeros")
+        nc.vector.memset(zeros[:], 0.0)
+        warm_ps = psum.tile([P, BANK], F32, name="warm_ps")
+        for i in range(WARM_UP_MATMULS):
+            nc.tensor.matmul(warm_ps[:], zeros[:, 0:P], zeros[:])
 
         fea_bf16 = held.tile([P, H_BLOCKS, N], BF16, name="fea_bf16")
         fea_f32 = held.tile([P, H_BLOCKS, N], F32, name="fea_f32")

@@ -11,8 +11,6 @@ H = 256
 R = 512
 H_BLOCKS = H // P
 R_BLOCKS = R // P
-BANK = 512
-WARM_UP_MATMULS = 6
 
 FLOPS = 2 * P * H * N + 2 * H * R * N
 
@@ -39,27 +37,24 @@ def tile_mutiheadattn_kernel(tc, table, dr_w, dr_b, w2, w2_b, offs, out):
         dr_b_sb = held.tile([P, H_BLOCKS], F32, name="dr_b_sb")
         w2_sb = held.tile([P, H_BLOCKS, R], BF16, name="w2_sb")
         w2_b_sb = held.tile([P, R_BLOCKS], F32, name="w2_b_sb")
-        w2_blocks = w2.rearrange("(b p) r -> b p r", p=P)
+        w2_by_block = w2.rearrange("(b p) r -> b p r", p=P)
 
         nc.sync.dma_start(offsets[:], offs)
         nc.scalar.dma_start(dr_w_sb[:], dr_w)
         nc.sync.dma_start(table_sb[:], table)
-        with nc.allow_non_contiguous_dma(reason="a bias: one float32 to a partition"):
+        with nc.allow_non_contiguous_dma(reason="dr_b: one float32 to a partition and block"):
             nc.scalar.dma_start(dr_b_sb[:], dr_b.rearrange("(b p) one -> p (b one)", p=P))
-        nc.sync.dma_start(w2_sb[:, 0, :], w2_blocks[0])
-        nc.scalar.dma_start(w2_sb[:, 1, :], w2_blocks[1])
-        with nc.allow_non_contiguous_dma(reason="a bias: one float32 to a partition"):
-            nc.scalar.dma_start(w2_b_sb[:], w2_b.rearrange("(c p) one -> p (c one)", p=P))
+        nc.sync.dma_start(w2_sb[:, 0, :], w2_by_block[0])
+        nc.scalar.dma_start(w2_sb[:, 1, :], w2_by_block[1])
+        nc.scalar.dma_start(w2_b_sb[:], w2_b.rearrange("(p c) one -> p (c one)", c=R_BLOCKS))
+
+        w2_by_blocks = w2_sb[:].rearrange("h b (p c) -> h b c p", c=R_BLOCKS)
+        fea_rows = out[0:H, :].rearrange("(b p) j -> b p j", p=P)
+        q_rows = out[H : H + R, :].rearrange("(p c) j -> c p j", c=R_BLOCKS)
 
         scratch = held.tile([P, 1], F32, name="scratch")
         nc.vector.memset(scratch[:], 0.0)
         nc.scalar.activation(scratch[:], scratch[:], RELU)
-
-        zeros = held.tile([P, BANK], BF16, name="zeros")
-        nc.vector.memset(zeros[:], 0.0)
-        warm_ps = psum.tile([P, BANK], F32, name="warm_ps")
-        for i in range(WARM_UP_MATMULS):
-            nc.tensor.matmul(warm_ps[:], zeros[:, 0:P], zeros[:])
 
         fea_bf16 = held.tile([P, H_BLOCKS, N], BF16, name="fea_bf16")
         fea_f32 = held.tile([P, H_BLOCKS, N], F32, name="fea_f32")
@@ -70,7 +65,7 @@ def tile_mutiheadattn_kernel(tc, table, dr_w, dr_b, w2, w2_b, offs, out):
             )
             add_bias(nc, b, fea_bf16[:, b, :], fea_ps[:], dr_b_sb[:, b : b + 1], relu=True)
             add_bias(nc, b, fea_f32[:, b, :], fea_ps[:], dr_b_sb[:, b : b + 1], relu=True)
-            nc.sync.dma_start(out[b * P : (b + 1) * P, :], fea_f32[:, b, :])
+            nc.sync.dma_start(fea_rows[b], fea_f32[:, b, :])
 
         q_f32 = held.tile([P, R_BLOCKS, N], F32, name="q_f32")
         q_ps = [psum.tile([P, N], F32, name=f"q_ps{c}") for c in range(R_BLOCKS)]
@@ -78,11 +73,11 @@ def tile_mutiheadattn_kernel(tc, table, dr_w, dr_b, w2, w2_b, offs, out):
             for c in range(R_BLOCKS):
                 nc.tensor.matmul(
                     q_ps[c][:],
-                    w2_sb[:, b, c * P : (c + 1) * P],
+                    w2_by_blocks[:, b, c, :],
                     fea_bf16[:, b, :],
                     start=(b == 0),
                     stop=(b == H_BLOCKS - 1),
                 )
         for c in range(R_BLOCKS):
             add_bias(nc, c, q_f32[:, c, :], q_ps[c][:], w2_b_sb[:, c : c + 1], relu=False)
-            nc.sync.dma_start(out[H + c * P : H + (c + 1) * P, :], q_f32[:, c, :])
+            nc.sync.dma_start(q_rows[c], q_f32[:, c, :])

@@ -25,6 +25,13 @@ def add_bias(nc, block, dst, src, bias, relu):
         nc.scalar.activation(dst, src, RELU if relu else IDENTITY, bias=bias)
 
 
+def store(nc, block, dst, src):
+    if block % 2 == 0:
+        nc.sync.dma_start(dst, src)
+    else:
+        nc.scalar.dma_start(dst, src)
+
+
 def tile_mutiheadattn_kernel(tc, table, dr_w, dr_b, w2, w2_b, offs, out):
     nc = tc.nc
     with (
@@ -37,20 +44,17 @@ def tile_mutiheadattn_kernel(tc, table, dr_w, dr_b, w2, w2_b, offs, out):
         dr_b_sb = held.tile([P, H_BLOCKS], F32, name="dr_b_sb")
         w2_sb = held.tile([P, H_BLOCKS, R], BF16, name="w2_sb")
         w2_b_sb = held.tile([P, R_BLOCKS], F32, name="w2_b_sb")
-        w2_by_block = w2.rearrange("(b p) r -> b p r", p=P)
+        w2_blocks = w2.rearrange("(b p) r -> b p r", p=P)
 
         nc.sync.dma_start(offsets[:], offs)
-        nc.scalar.dma_start(dr_w_sb[:], dr_w)
-        nc.sync.dma_start(table_sb[:], table)
-        with nc.allow_non_contiguous_dma(reason="dr_b: one float32 to a partition and block"):
+        nc.scalar.dma_start(table_sb[:], table)
+        nc.sync.dma_start(dr_w_sb[:], dr_w)
+        with nc.allow_non_contiguous_dma(reason="a bias: one float32 to a partition"):
             nc.scalar.dma_start(dr_b_sb[:], dr_b.rearrange("(b p) one -> p (b one)", p=P))
-        nc.sync.dma_start(w2_sb[:, 0, :], w2_by_block[0])
-        nc.scalar.dma_start(w2_sb[:, 1, :], w2_by_block[1])
-        nc.scalar.dma_start(w2_b_sb[:], w2_b.rearrange("(p c) one -> p (c one)", c=R_BLOCKS))
-
-        w2_by_blocks = w2_sb[:].rearrange("h b (p c) -> h b c p", c=R_BLOCKS)
-        fea_rows = out[0:H, :].rearrange("(b p) j -> b p j", p=P)
-        q_rows = out[H : H + R, :].rearrange("(p c) j -> c p j", c=R_BLOCKS)
+        nc.sync.dma_start(w2_sb[:, 0, :], w2_blocks[0])
+        nc.scalar.dma_start(w2_sb[:, 1, :], w2_blocks[1])
+        with nc.allow_non_contiguous_dma(reason="a bias: one float32 to a partition"):
+            nc.scalar.dma_start(w2_b_sb[:], w2_b.rearrange("(c p) one -> p (c one)", p=P))
 
         scratch = held.tile([P, 1], F32, name="scratch")
         nc.vector.memset(scratch[:], 0.0)
@@ -65,7 +69,7 @@ def tile_mutiheadattn_kernel(tc, table, dr_w, dr_b, w2, w2_b, offs, out):
             )
             add_bias(nc, b, fea_bf16[:, b, :], fea_ps[:], dr_b_sb[:, b : b + 1], relu=True)
             add_bias(nc, b, fea_f32[:, b, :], fea_ps[:], dr_b_sb[:, b : b + 1], relu=True)
-            nc.sync.dma_start(fea_rows[b], fea_f32[:, b, :])
+            store(nc, b, out[b * P : (b + 1) * P, :], fea_f32[:, b, :])
 
         q_f32 = held.tile([P, R_BLOCKS, N], F32, name="q_f32")
         q_ps = [psum.tile([P, N], F32, name=f"q_ps{c}") for c in range(R_BLOCKS)]
@@ -73,11 +77,11 @@ def tile_mutiheadattn_kernel(tc, table, dr_w, dr_b, w2, w2_b, offs, out):
             for c in range(R_BLOCKS):
                 nc.tensor.matmul(
                     q_ps[c][:],
-                    w2_by_blocks[:, b, c, :],
+                    w2_sb[:, b, c * P : (c + 1) * P],
                     fea_bf16[:, b, :],
                     start=(b == 0),
                     stop=(b == H_BLOCKS - 1),
                 )
         for c in range(R_BLOCKS):
             add_bias(nc, c, q_f32[:, c, :], q_ps[c][:], w2_b_sb[:, c : c + 1], relu=False)
-            nc.sync.dma_start(q_rows[c], q_f32[:, c, :])
+            store(nc, c, out[H + c * P : H + (c + 1) * P, :], q_f32[:, c, :])

@@ -11,6 +11,8 @@ H = 256
 R = 512
 H_BLOCKS = H // P
 R_BLOCKS = R // P
+WARM_UP_COLUMNS = 256
+WARM_UP_MATMULS = 7
 
 FLOPS = 2 * P * H * N + 2 * H * R * N
 
@@ -55,6 +57,12 @@ def tile_mutiheadattn_kernel(tc, table, dr_w, dr_b, w2, w2_b, offs, out):
         nc.scalar.dma_start(w2_sb[:, 1, :], w2_blocks[1])
         with nc.allow_non_contiguous_dma(reason="a bias: one float32 to a partition"):
             nc.scalar.dma_start(w2_b_sb[:], w2_b.rearrange("(c p) one -> p (c one)", p=P))
+
+        zeros = held.tile([P, WARM_UP_COLUMNS], BF16, name="zeros")
+        nc.vector.memset(zeros[:], 0.0)
+        warm_ps = psum.tile([P, WARM_UP_COLUMNS], F32, name="warm_ps")
+        for i in range(WARM_UP_MATMULS):
+            nc.tensor.matmul(warm_ps[:], zeros[:, 0:P], zeros[:])
 
         scratch = held.tile([P, 1], F32, name="scratch")
         nc.vector.memset(scratch[:], 0.0)

@@ -46,6 +46,7 @@ def tile_mutiheadattn_kernel(tc, table, dr_w, dr_b, w2, w2_b, offs, out):
         dr_b_sb = held.tile([P, H_BLOCKS], F32, name="dr_b_sb")
         w2_sb = held.tile([P, H_BLOCKS, R], BF16, name="w2_sb")
         w2_b_sb = held.tile([P, R_BLOCKS], F32, name="w2_b_sb")
+        q_rows = out[H:, :].rearrange("(p c) j -> c p j", c=R_BLOCKS)
         w2_blocks = w2.rearrange("(b p) r -> b p r", p=P)
 
         nc.sync.dma_start(offsets[:], offs)
@@ -55,8 +56,7 @@ def tile_mutiheadattn_kernel(tc, table, dr_w, dr_b, w2, w2_b, offs, out):
             nc.scalar.dma_start(dr_b_sb[:], dr_b.rearrange("(b p) one -> p (b one)", p=P))
         nc.sync.dma_start(w2_sb[:, 0, :], w2_blocks[0])
         nc.scalar.dma_start(w2_sb[:, 1, :], w2_blocks[1])
-        with nc.allow_non_contiguous_dma(reason="a bias: one float32 to a partition"):
-            nc.scalar.dma_start(w2_b_sb[:], w2_b.rearrange("(c p) one -> p (c one)", p=P))
+        nc.scalar.dma_start(w2_b_sb[:], w2_b.rearrange("(p c) one -> p (c one)", c=R_BLOCKS))
 
         zeros = held.tile([P, WARM_UP_COLUMNS], BF16, name="zeros")
         nc.vector.memset(zeros[:], 0.0)
@@ -85,11 +85,11 @@ def tile_mutiheadattn_kernel(tc, table, dr_w, dr_b, w2, w2_b, offs, out):
             for c in range(R_BLOCKS):
                 nc.tensor.matmul(
                     q_ps[c][:],
-                    w2_sb[:, b, c * P : (c + 1) * P],
+                    w2_sb[:, b, c::R_BLOCKS],
                     fea_bf16[:, b, :],
                     start=(b == 0),
                     stop=(b == H_BLOCKS - 1),
                 )
         for c in range(R_BLOCKS):
             add_bias(nc, c, q_f32[:, c, :], q_ps[c][:], w2_b_sb[:, c : c + 1], relu=False)
-            store(nc, c, out[H + c * P : H + (c + 1) * P, :], q_f32[:, c, :])
+            store(nc, c, q_rows[c], q_f32[:, c, :])

@@ -56,7 +56,7 @@ def tile_mutiheadattn_kernel(tc, table, dr_w, dr_b, w2, w2_b, offs, out):
             nc.scalar.dma_start(dr_b_sb[:], dr_b.rearrange("(b p) one -> p (b one)", p=P))
         nc.sync.dma_start(w2_sb[:, 0, :], w2_blocks[0])
         nc.scalar.dma_start(w2_sb[:, 1, :], w2_blocks[1])
-        nc.scalar.dma_start(w2_b_sb[:], w2_b.rearrange("(p c) one -> p (c one)", c=R_BLOCKS))
+        nc.gpsimd.dma_start(w2_b_sb[:], w2_b.rearrange("(p c) one -> p (c one)", c=R_BLOCKS))
 
         zeros = held.tile([P, WARM_UP_COLUMNS], BF16, name="zeros")
         nc.vector.memset(zeros[:], 0.0)

@@ -47,13 +47,13 @@ def tile_mutiheadattn_kernel(tc, table, dr_w, dr_b, w2, w2_b, offs, out):
         w2_sb = held.tile([P, H_BLOCKS, R], BF16, name="w2_sb")
         w2_b_sb = held.tile([P, R_BLOCKS], F32, name="w2_b_sb")
         q_rows = out[H:, :].rearrange("(p c) j -> c p j", c=R_BLOCKS)
-        w2_blocks = w2.rearrange("(b p) r -> b p r", p=P)
+        w2_blocks = w2.rearrange("(p b) r -> b p r", b=H_BLOCKS)
+        fea_rows = out[0:H, :].rearrange("(p b) j -> b p j", b=H_BLOCKS)
 
         nc.sync.dma_start(offsets[:], offs)
         nc.scalar.dma_start(table_sb[:], table)
         nc.sync.dma_start(dr_w_sb[:], dr_w)
-        with nc.allow_non_contiguous_dma(reason="a bias: one float32 to a partition"):
-            nc.scalar.dma_start(dr_b_sb[:], dr_b.rearrange("(b p) one -> p (b one)", p=P))
+        nc.scalar.dma_start(dr_b_sb[:], dr_b.rearrange("(p b) one -> p (b one)", b=H_BLOCKS))
         nc.sync.dma_start(w2_sb[:, 0, :], w2_blocks[0])
         nc.scalar.dma_start(w2_sb[:, 1, :], w2_blocks[1])
         nc.gpsimd.dma_start(w2_b_sb[:], w2_b.rearrange("(p c) one -> p (c one)", c=R_BLOCKS))
@@ -73,11 +73,13 @@ def tile_mutiheadattn_kernel(tc, table, dr_w, dr_b, w2, w2_b, offs, out):
         for b in range(H_BLOCKS):
             fea_ps = psum.tile([P, N], F32, name=f"fea_ps{b}")
             nc.tensor.matmul(
-                fea_ps[:], dr_w_sb[:, b * P : (b + 1) * P], table_sb[:].indirect(offsets[:])
+                fea_ps[:],
+                dr_w_sb[:, b::H_BLOCKS],
+                table_sb[:].indirect(offsets[:]),
             )
             add_bias(nc, b, fea_bf16[:, b, :], fea_ps[:], dr_b_sb[:, b : b + 1], relu=True)
             add_bias(nc, b, fea_f32[:, b, :], fea_ps[:], dr_b_sb[:, b : b + 1], relu=True)
-            store(nc, b, out[b * P : (b + 1) * P, :], fea_f32[:, b, :])
+            store(nc, b, fea_rows[b], fea_f32[:, b, :])
 
         q_f32 = held.tile([P, R_BLOCKS, N], F32, name="q_f32")
         q_ps = [psum.tile([P, N], F32, name=f"q_ps{c}") for c in range(R_BLOCKS)]

@@ -44,18 +44,19 @@ def tile_mutiheadattn_kernel(tc, table, dr_w, dr_b, w2, w2_b, offs, out):
         table_sb = held.tile([P, V], BF16, name="table_sb")
         dr_w_sb = held.tile([P, H], BF16, name="dr_w_sb")
         dr_b_sb = held.tile([P, H_BLOCKS], F32, name="dr_b_sb")
-        w2_sb = held.tile([P, H_BLOCKS, R], BF16, name="w2_sb")
+        w2_sb = held.tile([P, H_BLOCKS * R], BF16, name="w2_sb")
         w2_b_sb = held.tile([P, R_BLOCKS], F32, name="w2_b_sb")
         q_rows = out[H:, :].rearrange("(p c) j -> c p j", c=R_BLOCKS)
-        w2_blocks = w2.rearrange("(p b) r -> b p r", b=H_BLOCKS)
+        w2_runs = w2.rearrange("(p b) r -> p (b r)", b=H_BLOCKS)
         fea_rows = out[0:H, :].rearrange("(p b) j -> b p j", b=H_BLOCKS)
 
         nc.sync.dma_start(offsets[:], offs)
         nc.scalar.dma_start(table_sb[:], table)
         nc.sync.dma_start(dr_w_sb[:], dr_w)
         nc.scalar.dma_start(dr_b_sb[:], dr_b.rearrange("(p b) one -> p (b one)", b=H_BLOCKS))
-        nc.sync.dma_start(w2_sb[:, 0, :], w2_blocks[0])
-        nc.scalar.dma_start(w2_sb[:, 1, :], w2_blocks[1])
+        split = (H + V + H_BLOCKS * R) // 2 - H
+        nc.sync.dma_start(w2_sb[:, :split], w2_runs[:, :split])
+        nc.scalar.dma_start(w2_sb[:, split:], w2_runs[:, split:])
         nc.gpsimd.dma_start(w2_b_sb[:], w2_b.rearrange("(p c) one -> p (c one)", c=R_BLOCKS))
 
         zeros = held.tile([P, WARM_UP_COLUMNS], BF16, name="zeros")
@@ -87,7 +88,7 @@ def tile_mutiheadattn_kernel(tc, table, dr_w, dr_b, w2, w2_b, offs, out):
             for c in range(R_BLOCKS):
                 nc.tensor.matmul(
                     q_ps[c][:],
-                    w2_sb[:, b, c::R_BLOCKS],
+                    w2_sb[:, b * R + c : (b + 1) * R : R_BLOCKS],
                     fea_bf16[:, b, :],
                     start=(b == 0),
                     stop=(b == H_BLOCKS - 1),

@@ -11,8 +11,8 @@ H = 256
 R = 512
 H_BLOCKS = H // P
 R_BLOCKS = R // P
-WARM_UP_COLUMNS = 256
-WARM_UP_MATMULS = 7
+HALF = N // 2
+WARM_UP_MATMULS = 14
 
 FLOPS = 2 * P * H * N + 2 * H * R * N
 
@@ -59,11 +59,11 @@ def tile_mutiheadattn_kernel(tc, table, dr_w, dr_b, w2, w2_b, offs, out):
         nc.scalar.dma_start(w2_sb[:, split:], w2_runs[:, split:])
         nc.gpsimd.dma_start(w2_b_sb[:], w2_b.rearrange("(p c) one -> p (c one)", c=R_BLOCKS))
 
-        zeros = held.tile([P, WARM_UP_COLUMNS], BF16, name="zeros")
+        zeros = held.tile([P, N], BF16, name="zeros")
         nc.vector.memset(zeros[:], 0.0)
-        warm_ps = psum.tile([P, WARM_UP_COLUMNS], F32, name="warm_ps")
+        q_ps = [psum.tile([P, N], F32, name=f"q_ps{c}") for c in range(R_BLOCKS)]
         for i in range(WARM_UP_MATMULS):
-            nc.tensor.matmul(warm_ps[:], zeros[:, 0:P], zeros[:])
+            nc.tensor.matmul(q_ps[R_BLOCKS - 1][:], zeros[:], zeros[:])
 
         scratch = held.tile([P, 1], F32, name="scratch")
         nc.vector.memset(scratch[:], 0.0)
@@ -71,28 +71,33 @@ def tile_mutiheadattn_kernel(tc, table, dr_w, dr_b, w2, w2_b, offs, out):
 
         fea_bf16 = held.tile([P, H_BLOCKS, N], BF16, name="fea_bf16")
         fea_f32 = held.tile([P, H_BLOCKS, N], F32, name="fea_f32")
+        pieces = []
         for b in range(H_BLOCKS):
-            fea_ps = psum.tile([P, N], F32, name=f"fea_ps{b}")
-            nc.tensor.matmul(
-                fea_ps[:],
-                dr_w_sb[:, b::H_BLOCKS],
-                table_sb[:].indirect(offsets[:]),
-            )
-            add_bias(nc, b, fea_bf16[:, b, :], fea_ps[:], dr_b_sb[:, b : b + 1], relu=True)
-            add_bias(nc, b, fea_f32[:, b, :], fea_ps[:], dr_b_sb[:, b : b + 1], relu=True)
+            for i in range(2):
+                fea_ps = psum.tile([P, HALF], F32, name=f"fea_ps{b}_{i}")
+                nc.tensor.matmul(
+                    fea_ps[:],
+                    dr_w_sb[:, b::H_BLOCKS],
+                    table_sb[:].indirect(offsets[:, i * HALF // 16 : (i + 1) * HALF // 16]),
+                )
+                pieces.append((b, i, slice(i * HALF, (i + 1) * HALF), fea_ps))
+        for copy in (fea_bf16, fea_f32):
+            for b, i, words, fea_ps in pieces:
+                add_bias(nc, i, copy[:, b, words], fea_ps[:], dr_b_sb[:, b : b + 1], relu=True)
+        for b in range(H_BLOCKS):
             store(nc, b, fea_rows[b], fea_f32[:, b, :])
 
         q_f32 = held.tile([P, R_BLOCKS, N], F32, name="q_f32")
-        q_ps = [psum.tile([P, N], F32, name=f"q_ps{c}") for c in range(R_BLOCKS)]
-        for b in range(H_BLOCKS):
-            for c in range(R_BLOCKS):
-                nc.tensor.matmul(
-                    q_ps[c][:],
-                    w2_sb[:, b * R + c : (b + 1) * R : R_BLOCKS],
-                    fea_bf16[:, b, :],
-                    start=(b == 0),
-                    stop=(b == H_BLOCKS - 1),
-                )
+        for first in range(0, R_BLOCKS, 2):
+            for b in range(H_BLOCKS):
+                for c in (first, first + 1):
+                    nc.tensor.matmul(
+                        q_ps[c][:],
+                        w2_sb[:, b * R + c : (b + 1) * R : R_BLOCKS],
+                        fea_bf16[:, b, :],
+                        start=(b == 0),
+                        stop=(b == H_BLOCKS - 1),
+                    )
         for c in range(R_BLOCKS):
             add_bias(nc, c, q_f32[:, c, :], q_ps[c][:], w2_b_sb[:, c : c + 1], relu=False)
             store(nc, c, q_rows[c], q_f32[:, c, :])

import concourse.mybir as mybir

BF16, F32, U16 = mybir.dt.bfloat16, mybir.dt.float32, mybir.dt.uint16
ADD, MAX = mybir.AluOpType.add, mybir.AluOpType.max
RELU, IDENTITY = mybir.ActivationFunctionType.Relu, mybir.ActivationFunctionType.Identity

P = 128
V = 512
N = 128
H = 256
R = 512
H_BLOCKS = H // P
R_BLOCKS = R // P
HALF = N // 2
WARM_UP_MATMULS = 14

FLOPS = 2 * P * H * N + 2 * H * R * N


def add_bias(nc, block, dst, src, bias, relu):
    if block % 2 == 0:
        if relu:
            nc.vector.tensor_scalar(dst, src, bias, 0.0, ADD, MAX)
        else:
            nc.vector.tensor_scalar(dst, src, bias, None, ADD)
    else:
        nc.scalar.activation(dst, src, RELU if relu else IDENTITY, bias=bias)


def store(nc, block, dst, src):
    if block % 2 == 0:
        nc.sync.dma_start(dst, src)
    else:
        nc.scalar.dma_start(dst, src)


def tile_mutiheadattn_kernel(tc, table, dr_w, dr_b, w2, w2_b, offs, out):
    nc = tc.nc
    with (
        tc.tile_pool(name="held", bufs=1) as held,
        tc.psum_pool(name="psum", bufs=1) as psum,
    ):
        offsets = held.tile([P, N // 16], U16, name="offsets")
        table_sb = held.tile([P, V], BF16, name="table_sb")
        dr_w_sb = held.tile([P, H], BF16, name="dr_w_sb")
        dr_b_sb = held.tile([P, H_BLOCKS], F32, name="dr_b_sb")
        w2_sb = held.tile([P, H_BLOCKS * R], BF16, name="w2_sb")
        w2_b_sb = held.tile([P, R_BLOCKS], F32, name="w2_b_sb")
        q_rows = out[H:, :].rearrange("(p c) j -> c p j", c=R_BLOCKS)
        w2_runs = w2.rearrange("(p b) r -> p (b r)", b=H_BLOCKS)
        fea_rows = out[0:H, :].rearrange("(p b) j -> b p j", b=H_BLOCKS)

        nc.sync.dma_start(offsets[:], offs)
        nc.scalar.dma_start(table_sb[:], table)
        nc.sync.dma_start(dr_w_sb[:], dr_w)
        nc.scalar.dma_start(dr_b_sb[:], dr_b.rearrange("(p b) one -> p (b one)", b=H_BLOCKS))
        split = (H + V + H_BLOCKS * R) // 2 - H
        nc.sync.dma_start(w2_sb[:, :split], w2_runs[:, :split])
        nc.scalar.dma_start(w2_sb[:, split:], w2_runs[:, split:])
        nc.gpsimd.dma_start(w2_b_sb[:], w2_b.rearrange("(p c) one -> p (c one)", c=R_BLOCKS))

        zeros = held.tile([P, N], BF16, name="zeros")
        nc.vector.memset(zeros[:], 0.0)
        q_ps = [psum.tile([P, N], F32, name=f"q_ps{c}") for c in range(R_BLOCKS)]
        for i in range(WARM_UP_MATMULS):
            nc.tensor.matmul(q_ps[R_BLOCKS - 1][:], zeros[:], zeros[:])

        scratch = held.tile([P, 1], F32, name="scratch")
        nc.vector.memset(scratch[:], 0.0)
        nc.scalar.activation(scratch[:], scratch[:], RELU)

        fea_bf16 = held.tile([P, H_BLOCKS, N], BF16, name="fea_bf16")
        fea_f32 = held.tile([P, H_BLOCKS, N], F32, name="fea_f32")
        pieces = []
        for b in range(H_BLOCKS):
            for i in range(2):
                fea_ps = psum.tile([P, HALF], F32, name=f"fea_ps{b}_{i}")
                nc.tensor.matmul(
                    fea_ps[:],
                    dr_w_sb[:, b::H_BLOCKS],
                    table_sb[:].indirect(offsets[:, i * HALF // 16 : (i + 1) * HALF // 16]),
                )
                pieces.append((b, i, slice(i * HALF, (i + 1) * HALF), fea_ps))
        for copy in (fea_bf16, fea_f32):
            for b, i, words, fea_ps in pieces:
                add_bias(nc, i, copy[:, b, words], fea_ps[:], dr_b_sb[:, b : b + 1], relu=True)
        for b in range(H_BLOCKS):
            store(nc, b, fea_rows[b], fea_f32[:, b, :])

        q_f32 = held.tile([P, R_BLOCKS, N], F32, name="q_f32")
        for first in range(0, R_BLOCKS, 2):
            for b in range(H_BLOCKS):
                for c in (first, first + 1):
                    nc.tensor.matmul(
                        q_ps[c][:],
                        w2_sb[:, b * R + c : (b + 1) * R : R_BLOCKS],
                        fea_bf16[:, b, :],
                        start=(b == 0),
                        stop=(b == H_BLOCKS - 1),
                    )
        for c in range(R_BLOCKS):
            add_bias(nc, c, q_f32[:, c, :], q_ps[c][:], w2_b_sb[:, c : c + 1], relu=False)
            store(nc, c, q_rows[c], q_f32[:, c, :])
